import numpy as np
import ml_dtypes


def mxq(x, axis, fmt="e4m3"):
    dtype, down = {"e4m3": (ml_dtypes.float8_e4m3fn, 7), "e5m2": (ml_dtypes.float8_e5m2, 14)}[fmt]
    v = np.moveaxis(np.asarray(x, np.float32).astype(ml_dtypes.bfloat16).astype(np.float64), axis, -1)
    blocks = v.reshape(v.shape[:-1] + (-1, 32))
    amax = np.abs(blocks).max(-1, keepdims=True)
    byte = np.maximum(np.where(amax > 0, np.frexp(amax)[1] - 1 + 127, 0) - down, 1)
    scale = np.exp2(byte - 127.0)
    codes = (blocks / scale).astype(np.float32).astype(dtype).astype(np.float64)
    return np.moveaxis((codes * scale).reshape(v.shape), -1, axis)


WIDE = False


def mx_kscale(k):
    if not WIDE:
        return np.ones(k)
    levels = np.array([10, -10, 5, -5, 0])
    a = np.random.permutation(np.resize(levels, k // 512 * 4)).reshape(k // 512, 4)
    idx = np.arange(k)
    return np.exp2(a[idx // 512, idx % 128 // 32])


BF16 = ml_dtypes.bfloat16


def bf(x):
    return np.asarray(x, np.float32).astype(BF16)


def f64(x):
    return np.asarray(x).astype(np.float64)


E2M1 = np.array([0.0, 0.5, 1.0, 1.5, 2.0, 3.0, 4.0, 6.0, -0.0, -0.5, -1.0, -1.5, -2.0, -3.0, -4.0, -6.0])


def pack_weight(w, fmt):
    k, n = w.shape
    w = f64(bf(w)).reshape(k // 32, 32, n)
    amax = np.abs(w).max(1)
    if fmt == "e4m3":
        byte = np.frexp(amax)[1] - 1 + 127 - 7
    else:
        mant, ex = np.frexp(amax / 6.0)
        byte = np.where(mant > 0.5, ex, ex - 1) + 127
    byte = np.clip(np.where(amax > 0, byte, 1), 1, 254)
    scaled = (w * np.exp2(127.0 - byte)[:, None, :]).reshape(k, n).astype(np.float32)
    by_word = np.ascontiguousarray(scaled.reshape(k // 512, 128, 4, n).transpose(0, 1, 3, 2))
    if fmt == "e4m3":
        words = by_word.astype(ml_dtypes.float8_e4m3fn).view(np.uint8)
    else:
        c = by_word.astype(ml_dtypes.float4_e2m1fn).view(np.uint8) & 0xF
        words = c[..., 0::2] | (c[..., 1::2] << 4)
    return np.ascontiguousarray(words), np.ascontiguousarray(byte.astype(np.uint8).reshape(k // 512, 16, n))


def unpack_weight(words, scales, fmt):
    g, p, n, _ = words.shape
    if fmt == "e4m3":
        vals = np.ascontiguousarray(words).view(ml_dtypes.float8_e4m3fn).astype(np.float64)
    else:
        nib = np.empty((g, p, n, 4), np.uint8)
        nib[..., 0::2] = words & 0xF
        nib[..., 1::2] = words >> 4
        vals = E2M1[nib]
    vals = vals * np.repeat(np.exp2(scales.astype(np.float64) - 127.0), 8, axis=1)[..., None]
    return vals.transpose(0, 1, 3, 2).reshape(g * 512, n)

def pack4(w):
    words, scales = pack_weight(w, "e2m1")
    return words.reshape(words.shape[0], 128, -1), scales


def unpack4(words, scales):
    return unpack_weight(words.reshape(words.shape[0], 128, -1, 2), scales, "e2m1")


B, S, D, H, HS, R = 1, 256, 2048, 16, 128, 32
W = 3 * H * HS
HALF = R // 2
THETA = 10000.0


def rope_tables():
    inv = 1.0 / THETA ** (np.arange(0, R, 2) / R)
    pos = THETA - S + np.arange(S)
    ang = pos[:, None] * inv[None, :]
    return np.cos(ang), np.sin(ang)


def apply_rotary(t, cos, sin):
    re, im = t[..., :HALF], t[..., HALF:]
    c, sn = cos[None, :, None, :], sin[None, :, None, :]
    out = np.stack((re * c - im * sn, re * sn + im * c), axis=-1)
    return out.reshape(t.shape)


def setup_inputs():
    s = mx_kscale(D)
    cos, sin = rope_tables()
    x = bf(np.random.standard_normal((B, S, D)) * s)
    words, scales = pack4(np.random.standard_normal((D, W)) / np.sqrt(D) / s[:, None])
    b_qkv = bf(np.random.standard_normal(W) * 0.3)
    return {"x": x,
            "w_qkv_words": words, "w_qkv_scales": scales,
            "b_qkv": b_qkv,
            "cos": bf(cos), "sin": bf(sin)}


def reference(x, w_qkv_words, w_qkv_scales, b_qkv, cos, sin):
    cos, sin = f64(cos), f64(sin)
    qkv = (mxq(f64(x), 2, "e4m3") @ unpack4(w_qkv_words, w_qkv_scales)) + f64(b_qkv)
    qkv = qkv.reshape(B, S, H, 3 * HS)
    q, k, v = qkv[..., :HS], qkv[..., HS:2 * HS], qkv[..., 2 * HS:]
    q_rot = np.concatenate((apply_rotary(q[..., :R], cos, sin), q[..., R:]), axis=3)
    k_rot = np.concatenate((apply_rotary(k[..., :R], cos, sin), k[..., R:]), axis=3)
    return q_rot, k_rot, v

@@ -1,0 +1,223 @@
+from contextlib import ExitStack
+
+import concourse.mybir as mybir
+from concourse.masks import make_identity
+
+F32 = mybir.dt.float32
+BF16 = mybir.dt.bfloat16
+I32 = mybir.dt.int32
+U32 = mybir.dt.uint32
+U8 = mybir.dt.uint8
+FP8X4 = mybir.dt.float8_e4m3fn_x4
+FP4X4 = mybir.dt.float4_e2m1fn_x4
+ADD = mybir.AluOpType.add
+MULT = mybir.AluOpType.mult
+
+P = 128
+TOKENS = 256
+TOKEN_TILES = TOKENS // P
+D_MODEL = 2048
+K_PASS = 4 * P
+PASSES = D_MODEL // K_PASS
+HEADS = 16
+HEAD = 128
+PARTS = 3
+ROTARY = 32
+HALF = ROTARY // 2
+COLS = HEADS * PARTS * HEAD
+N_PASS = 512
+BLOCKS_PER_BANK = N_PASS // HEAD
+ROUND_HEADS = 4
+ROUNDS = HEADS // ROUND_HEADS
+ROUND_COLS = ROUND_HEADS * PARTS * HEAD
+ROUND_BANKS = ROUND_COLS // N_PASS
+SCALE_ROWS = K_PASS // 32
+
+FLOPS = 2 * TOKENS * D_MODEL * COLS
+
+
+def tile_gptneoxattention_pa_kernel(
+    tc, x, w_qkv_words, w_qkv_scales, b_qkv, cos, sin, out_0, out_1, out_2
+):
+    nc = tc.nc
+    outs = (out_0, out_1, out_2)
+
+    with ExitStack() as ctx:
+        keep = ctx.enter_context(tc.tile_pool(name="keep", bufs=1))
+        stages = ctx.enter_context(tc.tile_pool(name="stages", bufs=ROUNDS * TOKEN_TILES))
+        temps = ctx.enter_context(tc.tile_pool(name="temps", bufs=2))
+        psum = ctx.enter_context(tc.psum_pool(name="psum", bufs=8))
+        ctx.enter_context(tc.manual_schedule())
+
+        x_sb = keep.tile([P, TOKEN_TILES, D_MODEL], BF16)
+        for m in range(TOKEN_TILES):
+            nc.sync.dma_start(out=x_sb[:, m, :], in_=x[0, m * P : (m + 1) * P, :])
+
+        bias_rows = keep.tile([P, N_PASS], BF16)
+        nc.vector.memset(bias_rows[:], 0.0)
+        nc.scalar.dma_start(
+            out=bias_rows[0 : COLS // N_PASS, :], in_=b_qkv.rearrange("(c n) -> c n", n=N_PASS)
+        )
+        cos_sb = keep.tile([P, TOKEN_TILES, HALF], BF16)
+        sin_sb = keep.tile([P, TOKEN_TILES, HALF], BF16)
+        nc.scalar.dma_start(out=cos_sb[:], in_=cos.rearrange("(m p) j -> p m j", p=P))
+        nc.scalar.dma_start(out=sin_sb[:], in_=sin.rearrange("(m p) j -> p m j", p=P))
+
+        ident_bf16 = keep.tile([P, P], BF16)
+        make_identity(nc, ident_bf16[:])
+        ident_f32 = keep.tile([P, P], F32)
+        make_identity(nc, ident_f32[:])
+
+        words_view = w_qkv_words.bitcast(I32).rearrange("g p b -> p g b")
+        scales_view = w_qkv_scales.bitcast(I32).rearrange("g q n -> q g n")
+        w_words = []
+        w_scales = []
+        for r in range(ROUNDS):
+            plane = keep.tile([P, PASSES, ROUND_COLS], U8, name="w_scales%d" % r, align_bytes=64)
+            plane_i32 = plane[:].bitcast(I32)
+            nc.vector.memset(plane_i32, 0)
+            n_lo = r * ROUND_COLS // 4
+            n_hi = (r + 1) * ROUND_COLS // 4
+            for row in range(SCALE_ROWS // 2):
+                first = 32 * (row // 4) + row % 4
+                nc.sync.dma_start(
+                    out=plane_i32[first : P : 64, :, :], in_=scales_view[row : SCALE_ROWS : 8, :, n_lo:n_hi]
+                )
+            w_scales.append(plane)
+
+            words = keep.tile([P, PASSES, 2 * ROUND_COLS], U8, name="w_words%d" % r, align_bytes=64)
+            words_i32 = words[:].bitcast(I32)
+            pieces = ROUND_BANKS if r == 0 else 1
+            width = 2 * ROUND_COLS // 4 // pieces
+            for piece in range(pieces):
+                lo = piece * width
+                src = r * 2 * ROUND_COLS // 4 + lo
+                nc.sync.dma_start(
+                    out=words_i32[:, :, lo : lo + width], in_=words_view[:, :, src : src + width]
+                )
+            w_words.append(words)
+
+        with_re = keep.tile([P, TOKEN_TILES, HALF, 2], F32)
+        with_im = keep.tile([P, TOKEN_TILES, HALF, 2], F32)
+        nc.gpsimd.tensor_copy(out=with_re[:, :, :, 0], in_=cos_sb[:])
+        nc.gpsimd.tensor_copy(out=with_re[:, :, :, 1], in_=sin_sb[:])
+        nc.gpsimd.tensor_scalar_mul(out=with_im[:, :, :, 0], in0=sin_sb[:], scalar1=-1.0)
+        nc.gpsimd.tensor_copy(out=with_im[:, :, :, 1], in_=cos_sb[:])
+
+        bias_sb = keep.tile([P, COLS], BF16)
+
+        def broadcast_bias(r):
+            for bank in range(r * ROUND_BANKS, (r + 1) * ROUND_BANKS):
+                spread = psum.tile([P, N_PASS], BF16, tag="bank")
+                nc.tensor.matmul(
+                    out=spread[:],
+                    lhsT=ident_bf16[:, bank : bank + 1].to_broadcast([P, P]),
+                    rhs=bias_rows[:],
+                    start=True,
+                    stop=True,
+                )
+                nc.scalar.copy(out=bias_sb[:, bank * N_PASS : (bank + 1) * N_PASS], in_=spread[:])
+
+        grouped = keep.tile([P, TOKEN_TILES, PASSES, P, 4], BF16, align_bytes=64)
+        x_codes = keep.tile([P, TOKEN_TILES, PASSES * P], U32, align_bytes=64)
+        x_scales = keep.tile([P, TOKEN_TILES, PASSES * P], U8, align_bytes=64)
+
+        def quantise_tokens(m):
+            x_pairs = x_sb[:, m, :].bitcast(F32)
+            grouped_pairs = grouped[:].bitcast(F32)
+            for half in range(2):
+                turned = psum.tile([P, 2, 2, P], F32, tag="bank")
+                for gg in range(2):
+                    g = 2 * half + gg
+                    for u in range(2):
+                        nc.tensor.transpose(
+                            turned[:, gg, u, :],
+                            x_pairs[:, (K_PASS // 2) * g + u : (K_PASS // 2) * (g + 1) : 2],
+                            ident_f32[:],
+                        )
+                copy = nc.vector.tensor_copy if half == 0 else nc.scalar.copy
+                copy(
+                    out=grouped_pairs[:, m, 2 * half : 2 * half + 2, :, :],
+                    in_=turned[:].rearrange("p g u t -> p g t u"),
+                )
+            nc.vector.quantize_mx(
+                out=x_codes[:, m, :].bitcast(FP8X4),
+                scales=x_scales[:, m, :],
+                in_=grouped[:, m, :, :, :].rearrange("p g t j -> p (g t j)"),
+            )
+
+        def project(r, m, stage):
+            for bank in range(ROUND_BANKS):
+                acc = psum.tile([P, N_PASS], F32, tag="bank")
+                for g in range(PASSES):
+                    nc.tensor.matmul_mx(
+                        out=acc[:],
+                        lhsT=x_codes[:, m, g * P : (g + 1) * P].bitcast(FP8X4),
+                        lhsT_scale=x_scales[:, m, g * P : (g + 1) * P],
+                        rhs=w_words[r][:, g, 2 * bank * N_PASS : 2 * (bank + 1) * N_PASS].bitcast(FP4X4),
+                        rhs_scale=w_scales[r][:, g, bank * N_PASS : (bank + 1) * N_PASS],
+                        start=(g == 0),
+                        stop=(g == PASSES - 1),
+                    )
+                block = bank * BLOCKS_PER_BANK
+                bank_end = block + BLOCKS_PER_BANK
+                while block < bank_end:
+                    head = block // PARTS
+                    part = block % PARTS
+                    count = min(PARTS - part, bank_end - block)
+                    lo = (block - bank * BLOCKS_PER_BANK) * HEAD
+                    col = r * ROUND_COLS + block * HEAD
+                    nc.vector.tensor_tensor(
+                        out=stage[:, part : part + count, head, :],
+                        in0=acc[:, lo : lo + count * HEAD].rearrange("p (c f) -> p c f", f=HEAD),
+                        in1=bias_sb[:, col : col + count * HEAD].rearrange("p (c f) -> p c f", f=HEAD),
+                        op=ADD,
+                    )
+                    block += count
+
+        def rotate(engine, m, stage):
+            blocks = 2 * ROUND_HEADS
+            shape = [P, blocks, HALF, 2]
+            qk = stage[:, 0:2, :, :].rearrange("p c h f -> p (c h) f")
+            from_re = temps.tile(shape, F32)
+            from_im = temps.tile(shape, F32)
+            engine.tensor_tensor(
+                out=from_re[:],
+                in0=qk[:, :, 0:HALF].unsqueeze(3).to_broadcast(shape),
+                in1=with_re[:, m, :, :].unsqueeze(1).to_broadcast(shape),
+                op=MULT,
+            )
+            engine.tensor_tensor(
+                out=from_im[:],
+                in0=qk[:, :, HALF:ROTARY].unsqueeze(3).to_broadcast(shape),
+                in1=with_im[:, m, :, :].unsqueeze(1).to_broadcast(shape),
+                op=MULT,
+            )
+            engine.tensor_tensor(
+                out=qk[:, :, 0:ROTARY].rearrange("p b (j e) -> p b j e", e=2),
+                in0=from_re[:],
+                in1=from_im[:],
+                op=ADD,
+            )
+
+        def store(r, m, stage, part):
+            nc.scalar.dma_start(
+                out=outs[part][0, m * P : (m + 1) * P, r * ROUND_HEADS : (r + 1) * ROUND_HEADS, :],
+                in_=stage[:, part, :, :],
+            )
+
+        broadcast_bias(0)
+        quantise_tokens(0)
+        broadcast_bias(1)
+        quantise_tokens(1)
+        for r in range(ROUNDS):
+            for m in range(TOKEN_TILES):
+                stage = stages.tile([P, PARTS, ROUND_HEADS, HEAD], F32)
+                project(r, m, stage)
+                store(r, m, stage, 2)
+                last = r == ROUNDS - 1 and m == TOKEN_TILES - 1
+                rotate(nc.vector if last else nc.gpsimd, m, stage)
+                store(r, m, stage, 0)
+                store(r, m, stage, 1)
+            if r + 2 < ROUNDS:
+                broadcast_bias(r + 2)

@@ -78,10 +78,9 @@ def tile_gptneoxattention_pa_kernel(
             nc.vector.memset(plane_i32, 0)
             n_lo = r * ROUND_COLS // 4
             n_hi = (r + 1) * ROUND_COLS // 4
-            for row in range(SCALE_ROWS // 2):
-                first = 32 * (row // 4) + row % 4
+            for row in range(4):
                 nc.sync.dma_start(
-                    out=plane_i32[first : P : 64, :, :], in_=scales_view[row : SCALE_ROWS : 8, :, n_lo:n_hi]
+                    out=plane_i32[row : P : 32, :, :], in_=scales_view[row : SCALE_ROWS : 4, :, n_lo:n_hi]
                 )
             w_scales.append(plane)
 
@@ -201,7 +200,7 @@ def tile_gptneoxattention_pa_kernel(
             )
 
         def store(r, m, stage, part):
-            nc.scalar.dma_start(
+            nc.sync.dma_start(
                 out=outs[part][0, m * P : (m + 1) * P, r * ROUND_HEADS : (r + 1) * ROUND_HEADS, :],
                 in_=stage[:, part, :, :],
             )

@@ -78,9 +78,10 @@ def tile_gptneoxattention_pa_kernel(
             nc.vector.memset(plane_i32, 0)
             n_lo = r * ROUND_COLS // 4
             n_hi = (r + 1) * ROUND_COLS // 4
-            for row in range(4):
+            for row in range(SCALE_ROWS // 2):
+                first = 32 * (row // 4) + row % 4
                 nc.sync.dma_start(
-                    out=plane_i32[row : P : 32, :, :], in_=scales_view[row : SCALE_ROWS : 4, :, n_lo:n_hi]
+                    out=plane_i32[first : P : 64, :, :], in_=scales_view[row : SCALE_ROWS : 8, :, n_lo:n_hi]
                 )
             w_scales.append(plane)
 

@@ -27,11 +27,13 @@ HALF = ROTARY // 2
 COLS = HEADS * PARTS * HEAD
 N_PASS = 512
 BLOCKS_PER_BANK = N_PASS // HEAD
+COL_BANKS = COLS // N_PASS
 ROUND_HEADS = 4
 ROUNDS = HEADS // ROUND_HEADS
 ROUND_COLS = ROUND_HEADS * PARTS * HEAD
 ROUND_BANKS = ROUND_COLS // N_PASS
 SCALE_ROWS = K_PASS // 32
+HEAD_BIAS_BANKS = 6
 
 FLOPS = 2 * TOKENS * D_MODEL * COLS
 
@@ -53,15 +55,14 @@ def tile_gptneoxattention_pa_kernel(
         for m in range(TOKEN_TILES):
             nc.sync.dma_start(out=x_sb[:, m, :], in_=x[0, m * P : (m + 1) * P, :])
 
-        bias_rows = keep.tile([P, N_PASS], BF16)
+        warm_in = keep.tile([P, 2], F32)
+        warm_out = keep.tile([P, 2], F32)
+        nc.vector.memset(warm_in[:], 0.0)
+        nc.scalar.copy(out=warm_out[:], in_=warm_in[:])
+
+        bias_rows = keep.tile([P, ROUND_COLS], BF16)
         nc.vector.memset(bias_rows[:], 0.0)
-        nc.scalar.dma_start(
-            out=bias_rows[0 : COLS // N_PASS, :], in_=b_qkv.rearrange("(c n) -> c n", n=N_PASS)
-        )
-        cos_sb = keep.tile([P, TOKEN_TILES, HALF], BF16)
-        sin_sb = keep.tile([P, TOKEN_TILES, HALF], BF16)
-        nc.scalar.dma_start(out=cos_sb[:], in_=cos.rearrange("(m p) j -> p m j", p=P))
-        nc.scalar.dma_start(out=sin_sb[:], in_=sin.rearrange("(m p) j -> p m j", p=P))
+        nc.scalar.dma_start(out=bias_rows[0:ROUNDS, :], in_=b_qkv.rearrange("(r n) -> r n", n=ROUND_COLS))
 
         ident_bf16 = keep.tile([P, P], BF16)
         make_identity(nc, ident_bf16[:])
@@ -72,57 +73,62 @@ def tile_gptneoxattention_pa_kernel(
         scales_view = w_qkv_scales.bitcast(I32).rearrange("g q n -> q g n")
         w_words = []
         w_scales = []
-        for r in range(ROUNDS):
+
+        def load_scales(r, bank_lo, bank_hi):
+            plane_i32 = w_scales[r][:].bitcast(I32)
+            lo = bank_lo * N_PASS // 4
+            hi = bank_hi * N_PASS // 4
+            src = r * ROUND_COLS // 4
+            for row in range(4):
+                nc.sync.dma_start(
+                    out=plane_i32[row : P : 32, :, lo:hi], in_=scales_view[row : SCALE_ROWS : 4, :, src + lo : src + hi]
+                )
+
+        def load_words(r, bank_lo, bank_hi):
+            words_i32 = w_words[r][:].bitcast(I32)
+            lo = bank_lo * 2 * N_PASS // 4
+            hi = bank_hi * 2 * N_PASS // 4
+            src = r * 2 * ROUND_COLS // 4
+            nc.sync.dma_start(out=words_i32[:, :, lo:hi], in_=words_view[:, :, src + lo : src + hi])
+
+        def load_round(r, cuts):
             plane = keep.tile([P, PASSES, ROUND_COLS], U8, name="w_scales%d" % r, align_bytes=64)
-            plane_i32 = plane[:].bitcast(I32)
-            nc.vector.memset(plane_i32, 0)
-            n_lo = r * ROUND_COLS // 4
-            n_hi = (r + 1) * ROUND_COLS // 4
-            for row in range(SCALE_ROWS // 2):
-                first = 32 * (row // 4) + row % 4
-                nc.sync.dma_start(
-                    out=plane_i32[first : P : 64, :, :], in_=scales_view[row : SCALE_ROWS : 8, :, n_lo:n_hi]
-                )
+            nc.vector.memset(plane[:].bitcast(I32), 0)
             w_scales.append(plane)
-
             words = keep.tile([P, PASSES, 2 * ROUND_COLS], U8, name="w_words%d" % r, align_bytes=64)
-            words_i32 = words[:].bitcast(I32)
-            pieces = ROUND_BANKS if r == 0 else 1
-            width = 2 * ROUND_COLS // 4 // pieces
-            for piece in range(pieces):
-                lo = piece * width
-                src = r * 2 * ROUND_COLS // 4 + lo
-                nc.sync.dma_start(
-                    out=words_i32[:, :, lo : lo + width], in_=words_view[:, :, src : src + width]
-                )
             w_words.append(words)
+            for scale_cut, word_cuts in cuts:
+                load_scales(r, scale_cut[0], scale_cut[1])
+                for bank_lo, bank_hi in word_cuts:
+                    load_words(r, bank_lo, bank_hi)
 
-        with_re = keep.tile([P, TOKEN_TILES, HALF, 2], F32)
-        with_im = keep.tile([P, TOKEN_TILES, HALF, 2], F32)
-        nc.gpsimd.tensor_copy(out=with_re[:, :, :, 0], in_=cos_sb[:])
-        nc.gpsimd.tensor_copy(out=with_re[:, :, :, 1], in_=sin_sb[:])
-        nc.gpsimd.tensor_scalar_mul(out=with_im[:, :, :, 0], in0=sin_sb[:], scalar1=-1.0)
-        nc.gpsimd.tensor_copy(out=with_im[:, :, :, 1], in_=cos_sb[:])
+        load_round(0, [((0, 1), [(0, 1)]), ((1, 3), [(1, 2), (2, 3)])])
+        cos_sb = keep.tile([P, TOKEN_TILES, HALF], BF16)
+        sin_sb = keep.tile([P, TOKEN_TILES, HALF], BF16)
+        nc.gpsimd.dma_start(out=cos_sb[:], in_=cos.rearrange("(m p) j -> p m j", p=P))
+        nc.gpsimd.dma_start(out=sin_sb[:], in_=sin.rearrange("(m p) j -> p m j", p=P))
+        load_round(1, [((0, 3), [(0, 1), (1, 2), (2, 3)])])
 
         bias_sb = keep.tile([P, COLS], BF16)
 
-        def broadcast_bias(r):
-            for bank in range(r * ROUND_BANKS, (r + 1) * ROUND_BANKS):
-                spread = psum.tile([P, N_PASS], BF16, tag="bank")
-                nc.tensor.matmul(
-                    out=spread[:],
-                    lhsT=ident_bf16[:, bank : bank + 1].to_broadcast([P, P]),
-                    rhs=bias_rows[:],
-                    start=True,
-                    stop=True,
-                )
-                nc.scalar.copy(out=bias_sb[:, bank * N_PASS : (bank + 1) * N_PASS], in_=spread[:])
+        def broadcast_bias(c):
+            r = c // ROUND_BANKS
+            bank = c % ROUND_BANKS
+            spread = psum.tile([P, N_PASS], BF16, tag="bank")
+            nc.tensor.matmul(
+                out=spread[:],
+                lhsT=ident_bf16[:, r : r + 1].to_broadcast([P, P]),
+                rhs=bias_rows[:, bank * N_PASS : (bank + 1) * N_PASS],
+                start=True,
+                stop=True,
+            )
+            nc.scalar.copy(out=bias_sb[:, c * N_PASS : (c + 1) * N_PASS], in_=spread[:])
 
         grouped = keep.tile([P, TOKEN_TILES, PASSES, P, 4], BF16, align_bytes=64)
         x_codes = keep.tile([P, TOKEN_TILES, PASSES * P], U32, align_bytes=64)
         x_scales = keep.tile([P, TOKEN_TILES, PASSES * P], U8, align_bytes=64)
 
-        def quantise_tokens(m):
+        def turn_tokens(m):
             x_pairs = x_sb[:, m, :].bitcast(F32)
             grouped_pairs = grouped[:].bitcast(F32)
             for half in range(2):
@@ -135,66 +141,93 @@ def tile_gptneoxattention_pa_kernel(
                             x_pairs[:, (K_PASS // 2) * g + u : (K_PASS // 2) * (g + 1) : 2],
                             ident_f32[:],
                         )
-                copy = nc.vector.tensor_copy if half == 0 else nc.scalar.copy
+                copy = nc.scalar.copy if half == 0 else nc.vector.tensor_copy
                 copy(
                     out=grouped_pairs[:, m, 2 * half : 2 * half + 2, :, :],
                     in_=turned[:].rearrange("p g u t -> p g t u"),
                 )
-            nc.vector.quantize_mx(
-                out=x_codes[:, m, :].bitcast(FP8X4),
-                scales=x_scales[:, m, :],
-                in_=grouped[:, m, :, :, :].rearrange("p g t j -> p (g t j)"),
+
+        def quantise_tokens(m):
+            for half in range(2):
+                lo = 2 * half * P
+                hi = lo + 2 * P
+                nc.vector.quantize_mx(
+                    out=x_codes[:, m, lo:hi].bitcast(FP8X4),
+                    scales=x_scales[:, m, lo:hi],
+                    in_=grouped[:, m, 2 * half : 2 * half + 2, :, :].rearrange("p g t j -> p (g t j)"),
+                )
+
+        def project(c, m, stage):
+            r = c // ROUND_BANKS
+            bank = c % ROUND_BANKS
+            acc = psum.tile([P, N_PASS], F32, tag="bank")
+            for g in range(PASSES):
+                nc.tensor.matmul_mx(
+                    out=acc[:],
+                    lhsT=x_codes[:, m, g * P : (g + 1) * P].bitcast(FP8X4),
+                    lhsT_scale=x_scales[:, m, g * P : (g + 1) * P],
+                    rhs=w_words[r][:, g, 2 * bank * N_PASS : 2 * (bank + 1) * N_PASS].bitcast(FP4X4),
+                    rhs_scale=w_scales[r][:, g, bank * N_PASS : (bank + 1) * N_PASS],
+                    start=(g == 0),
+                    stop=(g == PASSES - 1),
+                )
+            block = bank * BLOCKS_PER_BANK
+            bank_end = block + BLOCKS_PER_BANK
+            while block < bank_end:
+                head = block // PARTS
+                part = block % PARTS
+                count = min(PARTS - part, bank_end - block)
+                lo = (block - bank * BLOCKS_PER_BANK) * HEAD
+                col = r * ROUND_COLS + block * HEAD
+                nc.vector.tensor_tensor(
+                    out=stage[:, part : part + count, head, :],
+                    in0=acc[:, lo : lo + count * HEAD].rearrange("p (c f) -> p c f", f=HEAD),
+                    in1=bias_sb[:, col : col + count * HEAD].rearrange("p (c f) -> p c f", f=HEAD),
+                    op=ADD,
+                )
+                block += count
+
+        def project_by_part(r, m, stage):
+            round_bias = bias_sb[:, r * ROUND_COLS : (r + 1) * ROUND_COLS].rearrange(
+                "p (h c f) -> p c h f", c=PARTS, f=HEAD
             )
+            for part in range(PARTS):
+                acc = psum.tile([P, ROUND_HEADS, HEAD], F32, tag="bank")
+                for head in range(ROUND_HEADS):
+                    col = (head * PARTS + part) * HEAD
+                    for g in range(PASSES):
+                        nc.tensor.matmul_mx(
+                            out=acc[:, head, :],
+                            lhsT=x_codes[:, m, g * P : (g + 1) * P].bitcast(FP8X4),
+                            lhsT_scale=x_scales[:, m, g * P : (g + 1) * P],
+                            rhs=w_words[r][:, g, 2 * col : 2 * (col + HEAD)].bitcast(FP4X4),
+                            rhs_scale=w_scales[r][:, g, col : col + HEAD],
+                            start=(g == 0),
+                            stop=(g == PASSES - 1),
+                        )
+                nc.vector.tensor_tensor(out=stage[:, part, :, :], in0=acc[:], in1=round_bias[:, part, :, :], op=ADD)
+                if part < 2:
+                    rotate(nc.vector, m, stage[:, part, :, :])
+                store(r, m, stage, part)
 
-        def project(r, m, stage):
-            for bank in range(ROUND_BANKS):
-                acc = psum.tile([P, N_PASS], F32, tag="bank")
-                for g in range(PASSES):
-                    nc.tensor.matmul_mx(
-                        out=acc[:],
-                        lhsT=x_codes[:, m, g * P : (g + 1) * P].bitcast(FP8X4),
-                        lhsT_scale=x_scales[:, m, g * P : (g + 1) * P],
-                        rhs=w_words[r][:, g, 2 * bank * N_PASS : 2 * (bank + 1) * N_PASS].bitcast(FP4X4),
-                        rhs_scale=w_scales[r][:, g, bank * N_PASS : (bank + 1) * N_PASS],
-                        start=(g == 0),
-                        stop=(g == PASSES - 1),
-                    )
-                block = bank * BLOCKS_PER_BANK
-                bank_end = block + BLOCKS_PER_BANK
-                while block < bank_end:
-                    head = block // PARTS
-                    part = block % PARTS
-                    count = min(PARTS - part, bank_end - block)
-                    lo = (block - bank * BLOCKS_PER_BANK) * HEAD
-                    col = r * ROUND_COLS + block * HEAD
-                    nc.vector.tensor_tensor(
-                        out=stage[:, part : part + count, head, :],
-                        in0=acc[:, lo : lo + count * HEAD].rearrange("p (c f) -> p c f", f=HEAD),
-                        in1=bias_sb[:, col : col + count * HEAD].rearrange("p (c f) -> p c f", f=HEAD),
-                        op=ADD,
-                    )
-                    block += count
-
-        def rotate(engine, m, stage):
-            blocks = 2 * ROUND_HEADS
-            shape = [P, blocks, HALF, 2]
-            qk = stage[:, 0:2, :, :].rearrange("p c h f -> p (c h) f")
-            from_re = temps.tile(shape, F32)
-            from_im = temps.tile(shape, F32)
+        def rotate(engine, m, blocks):
+            shape = [P, blocks.shape[1], HALF, 2]
+            from_re = temps.tile(shape, F32, tag="from_re")
+            from_im = temps.tile(shape, F32, tag="from_im")
             engine.tensor_tensor(
                 out=from_re[:],
-                in0=qk[:, :, 0:HALF].unsqueeze(3).to_broadcast(shape),
+                in0=blocks[:, :, 0:HALF].unsqueeze(3).to_broadcast(shape),
                 in1=with_re[:, m, :, :].unsqueeze(1).to_broadcast(shape),
                 op=MULT,
             )
             engine.tensor_tensor(
                 out=from_im[:],
-                in0=qk[:, :, HALF:ROTARY].unsqueeze(3).to_broadcast(shape),
+                in0=blocks[:, :, HALF:ROTARY].unsqueeze(3).to_broadcast(shape),
                 in1=with_im[:, m, :, :].unsqueeze(1).to_broadcast(shape),
                 op=MULT,
             )
             engine.tensor_tensor(
-                out=qk[:, :, 0:ROTARY].rearrange("p b (j e) -> p b j e", e=2),
+                out=blocks[:, :, 0:ROTARY].rearrange("p b (j e) -> p b j e", e=2),
                 in0=from_re[:],
                 in1=from_im[:],
                 op=ADD,
@@ -206,18 +239,48 @@ def tile_gptneoxattention_pa_kernel(
                 in_=stage[:, part, :, :],
             )
 
-        broadcast_bias(0)
-        quantise_tokens(0)
-        broadcast_bias(1)
-        quantise_tokens(1)
-        for r in range(ROUNDS):
+        per_run = HEAD_BIAS_BANKS // TOKEN_TILES
+        for m in range(TOKEN_TILES):
+            for c in range(m * per_run, (m + 1) * per_run):
+                broadcast_bias(c)
+            turn_tokens(m)
+            quantise_tokens(m)
+
+        load_round(2, [((0, 3), [(0, 3)])])
+        load_round(3, [((0, 3), [(0, 3)])])
+
+        with_re = keep.tile([P, TOKEN_TILES, HALF, 2], F32)
+        with_im = keep.tile([P, TOKEN_TILES, HALF, 2], F32)
+        nc.gpsimd.tensor_copy(out=with_re[:, :, :, 0], in_=cos_sb[:])
+        nc.gpsimd.tensor_copy(out=with_re[:, :, :, 1], in_=sin_sb[:])
+        nc.gpsimd.tensor_scalar_mul(out=with_im[:, :, :, 0], in0=sin_sb[:], scalar1=-1.0)
+        nc.gpsimd.tensor_copy(out=with_im[:, :, :, 1], in_=cos_sb[:])
+
+        def finish(r, m, stage):
+            store(r, m, stage, 2)
+            rotate(nc.gpsimd, m, stage[:, 0:2, :, :].rearrange("p c h f -> p (c h) f"))
+            store(r, m, stage, 0)
+            store(r, m, stage, 1)
+
+        first_stages = []
+        for m in range(TOKEN_TILES):
+            stage = stages.tile([P, PARTS, ROUND_HEADS, HEAD], F32, tag="stage")
+            first_stages.append(stage)
+        next_bias = HEAD_BIAS_BANKS
+        for bank in range(ROUND_BANKS):
             for m in range(TOKEN_TILES):
-                stage = stages.tile([P, PARTS, ROUND_HEADS, HEAD], F32)
-                project(r, m, stage)
-                store(r, m, stage, 2)
-                last = r == ROUNDS - 1 and m == TOKEN_TILES - 1
-                rotate(nc.vector if last else nc.gpsimd, m, stage)
-                store(r, m, stage, 0)
-                store(r, m, stage, 1)
-            if r + 2 < ROUNDS:
-                broadcast_bias(r + 2)
+                project(bank, m, first_stages[m])
+                broadcast_bias(next_bias)
+                next_bias += 1
+        for m in range(TOKEN_TILES):
+            finish(0, m, first_stages[m])
+
+        for r in range(1, ROUNDS):
+            for m in range(TOKEN_TILES):
+                stage = stages.tile([P, PARTS, ROUND_HEADS, HEAD], F32, tag="stage")
+                if r == ROUNDS - 1 and m == TOKEN_TILES - 1:
+                    project_by_part(r, m, stage)
+                else:
+                    for bank in range(ROUND_BANKS):
+                        project(r * ROUND_BANKS + bank, m, stage)
+                    finish(r, m, stage)

@@ -55,14 +55,14 @@ def tile_gptneoxattention_pa_kernel(
         for m in range(TOKEN_TILES):
             nc.sync.dma_start(out=x_sb[:, m, :], in_=x[0, m * P : (m + 1) * P, :])
 
+        bias_rows = keep.tile([P, ROUND_COLS], BF16)
+        nc.vector.memset(bias_rows[:], 0.0)
+        nc.scalar.dma_start(out=bias_rows[0:ROUNDS, :], in_=b_qkv.rearrange("(r n) -> r n", n=ROUND_COLS))
+
         warm_in = keep.tile([P, 2], F32)
         warm_out = keep.tile([P, 2], F32)
         nc.vector.memset(warm_in[:], 0.0)
         nc.scalar.copy(out=warm_out[:], in_=warm_in[:])
-
-        bias_rows = keep.tile([P, ROUND_COLS], BF16)
-        nc.vector.memset(bias_rows[:], 0.0)
-        nc.scalar.dma_start(out=bias_rows[0:ROUNDS, :], in_=b_qkv.rearrange("(r n) -> r n", n=ROUND_COLS))
 
         ident_bf16 = keep.tile([P, P], BF16)
         make_identity(nc, ident_bf16[:])

@@ -33,6 +33,7 @@ ROUNDS = HEADS // ROUND_HEADS
 ROUND_COLS = ROUND_HEADS * PARTS * HEAD
 ROUND_BANKS = ROUND_COLS // N_PASS
 SCALE_ROWS = K_PASS // 32
+FIRST_ROUND_ON_GPSIMD = 2
 HEAD_BIAS_BANKS = 6
 
 FLOPS = 2 * TOKENS * D_MODEL * COLS
@@ -71,18 +72,25 @@ def tile_gptneoxattention_pa_kernel(
 
         words_view = w_qkv_words.bitcast(I32).rearrange("g p b -> p g b")
         scales_view = w_qkv_scales.bitcast(I32).rearrange("g q n -> q g n")
+        scales_view_f32 = w_qkv_scales.bitcast(F32).rearrange("g q n -> q g n")
         w_words = []
         w_scales = []
 
         def load_scales(r, bank_lo, bank_hi):
-            plane_i32 = w_scales[r][:].bitcast(I32)
             lo = bank_lo * N_PASS // 4
             hi = bank_hi * N_PASS // 4
             src = r * ROUND_COLS // 4
             for row in range(4):
-                nc.sync.dma_start(
-                    out=plane_i32[row : P : 32, :, lo:hi], in_=scales_view[row : SCALE_ROWS : 4, :, src + lo : src + hi]
-                )
+                if r >= FIRST_ROUND_ON_GPSIMD:
+                    nc.gpsimd.dma_start(
+                        out=w_scales[r][:].bitcast(F32)[row : P : 32, :, lo:hi],
+                        in_=scales_view_f32[row : SCALE_ROWS : 4, :, src + lo : src + hi],
+                    )
+                else:
+                    nc.sync.dma_start(
+                        out=w_scales[r][:].bitcast(I32)[row : P : 32, :, lo:hi],
+                        in_=scales_view[row : SCALE_ROWS : 4, :, src + lo : src + hi],
+                    )
 
         def load_words(r, bank_lo, bank_hi):
             words_i32 = w_words[r][:].bitcast(I32)

from contextlib import ExitStack

import concourse.mybir as mybir
from concourse.masks import make_identity

F32 = mybir.dt.float32
BF16 = mybir.dt.bfloat16
I32 = mybir.dt.int32
U32 = mybir.dt.uint32
U8 = mybir.dt.uint8
FP8X4 = mybir.dt.float8_e4m3fn_x4
FP4X4 = mybir.dt.float4_e2m1fn_x4
ADD = mybir.AluOpType.add
MULT = mybir.AluOpType.mult

P = 128
TOKENS = 256
TOKEN_TILES = TOKENS // P
D_MODEL = 2048
K_PASS = 4 * P
PASSES = D_MODEL // K_PASS
HEADS = 16
HEAD = 128
PARTS = 3
ROTARY = 32
HALF = ROTARY // 2
COLS = HEADS * PARTS * HEAD
N_PASS = 512
BLOCKS_PER_BANK = N_PASS // HEAD
COL_BANKS = COLS // N_PASS
ROUND_HEADS = 4
ROUNDS = HEADS // ROUND_HEADS
ROUND_COLS = ROUND_HEADS * PARTS * HEAD
ROUND_BANKS = ROUND_COLS // N_PASS
SCALE_ROWS = K_PASS // 32
FIRST_ROUND_ON_GPSIMD = 2
HEAD_BIAS_BANKS = 6

FLOPS = 2 * TOKENS * D_MODEL * COLS


def tile_gptneoxattention_pa_kernel(
    tc, x, w_qkv_words, w_qkv_scales, b_qkv, cos, sin, out_0, out_1, out_2
):
    nc = tc.nc
    outs = (out_0, out_1, out_2)

    with ExitStack() as ctx:
        keep = ctx.enter_context(tc.tile_pool(name="keep", bufs=1))
        stages = ctx.enter_context(tc.tile_pool(name="stages", bufs=ROUNDS * TOKEN_TILES))
        temps = ctx.enter_context(tc.tile_pool(name="temps", bufs=2))
        psum = ctx.enter_context(tc.psum_pool(name="psum", bufs=8))
        ctx.enter_context(tc.manual_schedule())

        x_sb = keep.tile([P, TOKEN_TILES, D_MODEL], BF16)
        for m in range(TOKEN_TILES):
            nc.sync.dma_start(out=x_sb[:, m, :], in_=x[0, m * P : (m + 1) * P, :])

        bias_rows = keep.tile([P, ROUND_COLS], BF16)
        nc.vector.memset(bias_rows[:], 0.0)
        nc.scalar.dma_start(out=bias_rows[0:ROUNDS, :], in_=b_qkv.rearrange("(r n) -> r n", n=ROUND_COLS))

        warm_in = keep.tile([P, 2], F32)
        warm_out = keep.tile([P, 2], F32)
        nc.vector.memset(warm_in[:], 0.0)
        nc.scalar.copy(out=warm_out[:], in_=warm_in[:])

        ident_bf16 = keep.tile([P, P], BF16)
        make_identity(nc, ident_bf16[:])
        ident_f32 = keep.tile([P, P], F32)
        make_identity(nc, ident_f32[:])

        words_view = w_qkv_words.bitcast(I32).rearrange("g p b -> p g b")
        scales_view = w_qkv_scales.bitcast(I32).rearrange("g q n -> q g n")
        scales_view_f32 = w_qkv_scales.bitcast(F32).rearrange("g q n -> q g n")
        w_words = []
        w_scales = []

        def load_scales(r, bank_lo, bank_hi):
            lo = bank_lo * N_PASS // 4
            hi = bank_hi * N_PASS // 4
            src = r * ROUND_COLS // 4
            for row in range(4):
                if r >= FIRST_ROUND_ON_GPSIMD:
                    nc.gpsimd.dma_start(
                        out=w_scales[r][:].bitcast(F32)[row : P : 32, :, lo:hi],
                        in_=scales_view_f32[row : SCALE_ROWS : 4, :, src + lo : src + hi],
                    )
                else:
                    nc.sync.dma_start(
                        out=w_scales[r][:].bitcast(I32)[row : P : 32, :, lo:hi],
                        in_=scales_view[row : SCALE_ROWS : 4, :, src + lo : src + hi],
                    )

        def load_words(r, bank_lo, bank_hi):
            words_i32 = w_words[r][:].bitcast(I32)
            lo = bank_lo * 2 * N_PASS // 4
            hi = bank_hi * 2 * N_PASS // 4
            src = r * 2 * ROUND_COLS // 4
            nc.sync.dma_start(out=words_i32[:, :, lo:hi], in_=words_view[:, :, src + lo : src + hi])

        def load_round(r, cuts):
            plane = keep.tile([P, PASSES, ROUND_COLS], U8, name="w_scales%d" % r, align_bytes=64)
            nc.vector.memset(plane[:].bitcast(I32), 0)
            w_scales.append(plane)
            words = keep.tile([P, PASSES, 2 * ROUND_COLS], U8, name="w_words%d" % r, align_bytes=64)
            w_words.append(words)
            for scale_cut, word_cuts in cuts:
                load_scales(r, scale_cut[0], scale_cut[1])
                for bank_lo, bank_hi in word_cuts:
                    load_words(r, bank_lo, bank_hi)

        load_round(0, [((0, 1), [(0, 1)]), ((1, 3), [(1, 2), (2, 3)])])
        cos_sb = keep.tile([P, TOKEN_TILES, HALF], BF16)
        sin_sb = keep.tile([P, TOKEN_TILES, HALF], BF16)
        nc.gpsimd.dma_start(out=cos_sb[:], in_=cos.rearrange("(m p) j -> p m j", p=P))
        nc.gpsimd.dma_start(out=sin_sb[:], in_=sin.rearrange("(m p) j -> p m j", p=P))
        load_round(1, [((0, 3), [(0, 1), (1, 2), (2, 3)])])

        bias_sb = keep.tile([P, COLS], BF16)

        def broadcast_bias(c):
            r = c // ROUND_BANKS
            bank = c % ROUND_BANKS
            spread = psum.tile([P, N_PASS], BF16, tag="bank")
            nc.tensor.matmul(
                out=spread[:],
                lhsT=ident_bf16[:, r : r + 1].to_broadcast([P, P]),
                rhs=bias_rows[:, bank * N_PASS : (bank + 1) * N_PASS],
                start=True,
                stop=True,
            )
            nc.scalar.copy(out=bias_sb[:, c * N_PASS : (c + 1) * N_PASS], in_=spread[:])

        grouped = keep.tile([P, TOKEN_TILES, PASSES, P, 4], BF16, align_bytes=64)
        x_codes = keep.tile([P, TOKEN_TILES, PASSES * P], U32, align_bytes=64)
        x_scales = keep.tile([P, TOKEN_TILES, PASSES * P], U8, align_bytes=64)

        def turn_tokens(m):
            x_pairs = x_sb[:, m, :].bitcast(F32)
            grouped_pairs = grouped[:].bitcast(F32)
            for half in range(2):
                turned = psum.tile([P, 2, 2, P], F32, tag="bank")
                for gg in range(2):
                    g = 2 * half + gg
                    for u in range(2):
                        nc.tensor.transpose(
                            turned[:, gg, u, :],
                            x_pairs[:, (K_PASS // 2) * g + u : (K_PASS // 2) * (g + 1) : 2],
                            ident_f32[:],
                        )
                copy = nc.scalar.copy if half == 0 else nc.vector.tensor_copy
                copy(
                    out=grouped_pairs[:, m, 2 * half : 2 * half + 2, :, :],
                    in_=turned[:].rearrange("p g u t -> p g t u"),
                )

        def quantise_tokens(m):
            for half in range(2):
                lo = 2 * half * P
                hi = lo + 2 * P
                nc.vector.quantize_mx(
                    out=x_codes[:, m, lo:hi].bitcast(FP8X4),
                    scales=x_scales[:, m, lo:hi],
                    in_=grouped[:, m, 2 * half : 2 * half + 2, :, :].rearrange("p g t j -> p (g t j)"),
                )

        def project(c, m, stage):
            r = c // ROUND_BANKS
            bank = c % ROUND_BANKS
            acc = psum.tile([P, N_PASS], F32, tag="bank")
            for g in range(PASSES):
                nc.tensor.matmul_mx(
                    out=acc[:],
                    lhsT=x_codes[:, m, g * P : (g + 1) * P].bitcast(FP8X4),
                    lhsT_scale=x_scales[:, m, g * P : (g + 1) * P],
                    rhs=w_words[r][:, g, 2 * bank * N_PASS : 2 * (bank + 1) * N_PASS].bitcast(FP4X4),
                    rhs_scale=w_scales[r][:, g, bank * N_PASS : (bank + 1) * N_PASS],
                    start=(g == 0),
                    stop=(g == PASSES - 1),
                )
            block = bank * BLOCKS_PER_BANK
            bank_end = block + BLOCKS_PER_BANK
            while block < bank_end:
                head = block // PARTS
                part = block % PARTS
                count = min(PARTS - part, bank_end - block)
                lo = (block - bank * BLOCKS_PER_BANK) * HEAD
                col = r * ROUND_COLS + block * HEAD
                nc.vector.tensor_tensor(
                    out=stage[:, part : part + count, head, :],
                    in0=acc[:, lo : lo + count * HEAD].rearrange("p (c f) -> p c f", f=HEAD),
                    in1=bias_sb[:, col : col + count * HEAD].rearrange("p (c f) -> p c f", f=HEAD),
                    op=ADD,
                )
                block += count

        def project_by_part(r, m, stage):
            round_bias = bias_sb[:, r * ROUND_COLS : (r + 1) * ROUND_COLS].rearrange(
                "p (h c f) -> p c h f", c=PARTS, f=HEAD
            )
            for part in range(PARTS):
                acc = psum.tile([P, ROUND_HEADS, HEAD], F32, tag="bank")
                for head in range(ROUND_HEADS):
                    col = (head * PARTS + part) * HEAD
                    for g in range(PASSES):
                        nc.tensor.matmul_mx(
                            out=acc[:, head, :],
                            lhsT=x_codes[:, m, g * P : (g + 1) * P].bitcast(FP8X4),
                            lhsT_scale=x_scales[:, m, g * P : (g + 1) * P],
                            rhs=w_words[r][:, g, 2 * col : 2 * (col + HEAD)].bitcast(FP4X4),
                            rhs_scale=w_scales[r][:, g, col : col + HEAD],
                            start=(g == 0),
                            stop=(g == PASSES - 1),
                        )
                nc.vector.tensor_tensor(out=stage[:, part, :, :], in0=acc[:], in1=round_bias[:, part, :, :], op=ADD)
                if part < 2:
                    rotate(nc.vector, m, stage[:, part, :, :])
                store(r, m, stage, part)

        def rotate(engine, m, blocks):
            shape = [P, blocks.shape[1], HALF, 2]
            from_re = temps.tile(shape, F32, tag="from_re")
            from_im = temps.tile(shape, F32, tag="from_im")
            engine.tensor_tensor(
                out=from_re[:],
                in0=blocks[:, :, 0:HALF].unsqueeze(3).to_broadcast(shape),
                in1=with_re[:, m, :, :].unsqueeze(1).to_broadcast(shape),
                op=MULT,
            )
            engine.tensor_tensor(
                out=from_im[:],
                in0=blocks[:, :, HALF:ROTARY].unsqueeze(3).to_broadcast(shape),
                in1=with_im[:, m, :, :].unsqueeze(1).to_broadcast(shape),
                op=MULT,
            )
            engine.tensor_tensor(
                out=blocks[:, :, 0:ROTARY].rearrange("p b (j e) -> p b j e", e=2),
                in0=from_re[:],
                in1=from_im[:],
                op=ADD,
            )

        def store(r, m, stage, part):
            nc.sync.dma_start(
                out=outs[part][0, m * P : (m + 1) * P, r * ROUND_HEADS : (r + 1) * ROUND_HEADS, :],
                in_=stage[:, part, :, :],
            )

        per_run = HEAD_BIAS_BANKS // TOKEN_TILES
        for m in range(TOKEN_TILES):
            for c in range(m * per_run, (m + 1) * per_run):
                broadcast_bias(c)
            turn_tokens(m)
            quantise_tokens(m)

        load_round(2, [((0, 3), [(0, 3)])])
        load_round(3, [((0, 3), [(0, 3)])])

        with_re = keep.tile([P, TOKEN_TILES, HALF, 2], F32)
        with_im = keep.tile([P, TOKEN_TILES, HALF, 2], F32)
        nc.gpsimd.tensor_copy(out=with_re[:, :, :, 0], in_=cos_sb[:])
        nc.gpsimd.tensor_copy(out=with_re[:, :, :, 1], in_=sin_sb[:])
        nc.gpsimd.tensor_scalar_mul(out=with_im[:, :, :, 0], in0=sin_sb[:], scalar1=-1.0)
        nc.gpsimd.tensor_copy(out=with_im[:, :, :, 1], in_=cos_sb[:])

        def finish(r, m, stage):
            store(r, m, stage, 2)
            rotate(nc.gpsimd, m, stage[:, 0:2, :, :].rearrange("p c h f -> p (c h) f"))
            store(r, m, stage, 0)
            store(r, m, stage, 1)

        first_stages = []
        for m in range(TOKEN_TILES):
            stage = stages.tile([P, PARTS, ROUND_HEADS, HEAD], F32, tag="stage")
            first_stages.append(stage)
        next_bias = HEAD_BIAS_BANKS
        for bank in range(ROUND_BANKS):
            for m in range(TOKEN_TILES):
                project(bank, m, first_stages[m])
                broadcast_bias(next_bias)
                next_bias += 1
        for m in range(TOKEN_TILES):
            finish(0, m, first_stages[m])

        for r in range(1, ROUNDS):
            for m in range(TOKEN_TILES):
                stage = stages.tile([P, PARTS, ROUND_HEADS, HEAD], F32, tag="stage")
                if r == ROUNDS - 1 and m == TOKEN_TILES - 1:
                    project_by_part(r, m, stage)
                else:
                    for bank in range(ROUND_BANKS):
                        project(r * ROUND_BANKS + bank, m, stage)
                    finish(r, m, stage)
